import numpy as np
import ml_dtypes


def mxq(x, axis, fmt="e4m3"):
    dtype, down = {"e4m3": (ml_dtypes.float8_e4m3fn, 7), "e5m2": (ml_dtypes.float8_e5m2, 14)}[fmt]
    v = np.moveaxis(np.asarray(x, np.float32).astype(ml_dtypes.bfloat16).astype(np.float64), axis, -1)
    blocks = v.reshape(v.shape[:-1] + (-1, 32))
    amax = np.abs(blocks).max(-1, keepdims=True)
    byte = np.maximum(np.where(amax > 0, np.frexp(amax)[1] - 1 + 127, 0) - down, 1)
    scale = np.exp2(byte - 127.0)
    codes = (blocks / scale).astype(np.float32).astype(dtype).astype(np.float64)
    return np.moveaxis((codes * scale).reshape(v.shape), -1, axis)


WIDE = False


def mx_kscale(k):
    if not WIDE:
        return np.ones(k)
    levels = np.array([20, -20, 10, -10, 0])
    a = np.random.permutation(np.resize(levels, k // 512 * 4)).reshape(k // 512, 4)
    idx = np.arange(k)
    return np.exp2(a[idx // 512, idx % 128 // 32])


BF16 = ml_dtypes.bfloat16


def bf(x):
    return np.asarray(x, np.float32).astype(BF16)


def f64(x):
    return np.asarray(x).astype(np.float64)


B, I, H = 512, 1024, 1024


def sigmoid(v):
    return 1.0 / (1.0 + np.exp(-v))


def setup_inputs():
    s = mx_kscale(B)[:, None]
    x0 = bf(np.random.standard_normal((B, I)))
    hid = bf(np.random.standard_normal((B, H)))
    wx = bf(np.random.standard_normal((3, I, H)) * 0.6 / np.sqrt(I))
    wh = bf(np.random.standard_normal((3, H, H)) * 0.6 / np.sqrt(H))
    bx = bf(np.random.standard_normal((3, H)) * 0.3)
    bh = bf(np.random.standard_normal((3, H)) * 0.3)
    g = bf(np.random.standard_normal((B, H)) * np.exp2(np.random.randint(-12, 1, (B, 1))) * 4.0 / s)
    gx = f64(x0) @ f64(wx) + f64(bx)[:, None, :]
    gh = f64(hid) @ f64(wh) + f64(bh)[:, None, :]
    r = sigmoid(gx[0] + gh[0])
    z = sigmoid(gx[1] + gh[1])
    n = np.tanh(gx[2] + r * gh[2])
    gates = np.stack([r, z, n], axis=0)
    hn = gh[2]
    return {"x": bf(f64(x0) * s), "hid": hid, "wx": wx, "wh": wh, "bx": bx, "bh": bh,
            "gates": np.asarray(gates, np.float32), "hn": np.asarray(hn, np.float32), "grad_out": g}


def reference(x, hid, wx, wh, bx, bh, gates, hn, grad_out):
    x, hid, gates, hn, g = f64(x), f64(hid), f64(gates), f64(hn), f64(grad_out)
    r, z, n = gates[0], gates[1], gates[2]
    dn = g * (1.0 - z) * (1.0 - n * n)
    dz = g * (hid - n) * z * (1.0 - z)
    dr = dn * hn * r * (1.0 - r)
    d = np.stack([dr, dz, dn], axis=0)
    return mxq(x, 0, "e4m3").T @ mxq(d, 1, "e5m2")

@@ -1,0 +1,194 @@
+from contextlib import ExitStack
+
+import concourse.mybir as mybir
+
+F32 = mybir.dt.float32
+BF16 = mybir.dt.bfloat16
+U32 = mybir.dt.uint32
+U8 = mybir.dt.uint8
+E4M3_X4 = mybir.dt.float8_e4m3fn_x4
+E5M2_X4 = mybir.dt.float8_e5m2_x4
+ALU = mybir.AluOpType
+SQUARE = mybir.ActivationFunctionType.Square
+
+P = 128
+PACK = 4
+TOKENS = P * PACK
+IN_DIM = 1024
+HID_DIM = 1024
+GATE_R = 0
+GATE_Z = 1
+GATE_N = 2
+
+M_TILE = P
+N_TILE = 512
+M_TILES = IN_DIM // M_TILE
+HALVES = HID_DIM // N_TILE
+M_TILES_PER_STORE = 4
+
+TOKEN_PAIRS = (slice(0, 2), slice(2, 4))
+
+RUN = 4
+
+PLANE_SLOTS = 7
+STAGE_SLOTS = 6
+PSUM_BANKS = 8
+
+FLOPS = 2 * 3 * TOKENS * IN_DIM * HID_DIM
+BYTES = 3 * TOKENS * 1024 * 2 + 4 * TOKENS * 1024 * 4 + 3 * IN_DIM * HID_DIM * 4
+
+
+def token_rows(dram):
+    return dram.rearrange("(p j) c -> p j c", j=PACK)
+
+
+def read_regrouping(rows):
+    return rows.rearrange("p j (c i) -> p c j i", i=RUN)
+
+
+def write_regrouping(grouped):
+    return grouped.rearrange("p (c i) j -> p c j i", i=RUN)
+
+
+def tile_grucellv2_v_kernel(tc, x, hid, wx, wh, bx, bh, gates, hn, grad_out, out):
+    nc = tc.nc
+    out_tiles = out.rearrange("g (t m) h -> g m t h", m=M_TILE)
+
+    with ExitStack() as ctx:
+        narrow = ctx.enter_context(tc.tile_pool(name="narrow", bufs=1))
+        planes = ctx.enter_context(tc.tile_pool(name="planes", bufs=PLANE_SLOTS))
+        x_mx = ctx.enter_context(tc.tile_pool(name="x_mx", bufs=1))
+        d_mx = ctx.enter_context(tc.tile_pool(name="d_mx", bufs=3))
+        stage = ctx.enter_context(tc.tile_pool(name="stage", bufs=STAGE_SLOTS))
+        psum = ctx.enter_context(tc.psum_pool(name="psum", bufs=PSUM_BANKS))
+
+        def plane(name):
+            return planes.tile([P, PACK, HID_DIM], F32, name=name, tag="plane")
+
+        def load(rows_tile, dram):
+            for pair in TOKEN_PAIRS:
+                nc.sync.dma_start(out=rows_tile[:, pair, :], in_=token_rows(dram)[:, pair, :])
+
+        x_rows = narrow.tile([P, PACK, IN_DIM], BF16)
+        g_rows = narrow.tile([P, PACK, HID_DIM], BF16)
+        hid_rows = narrow.tile([P, PACK, HID_DIM], BF16)
+        z = plane("z")
+        n = plane("n")
+        r = plane("r")
+        hn_rows = plane("hn_rows")
+
+        nc.sync.dma_start(out=x_rows[:], in_=token_rows(x))
+        for pair in TOKEN_PAIRS:
+            nc.sync.dma_start(out=g_rows[:, pair, :], in_=token_rows(grad_out)[:, pair, :])
+            nc.sync.dma_start(out=z[:, pair, :], in_=token_rows(gates[GATE_Z, :, :])[:, pair, :])
+        load(n, gates[GATE_N, :, :])
+        nc.sync.dma_start(out=hid_rows[:], in_=token_rows(hid))
+        load(r, gates[GATE_R, :, :])
+        load(hn_rows, hn)
+
+        x_grouped = x_mx.tile([P, IN_DIM, PACK], BF16, align_bytes=64)
+        x_codes = x_mx.tile([P, IN_DIM], U32, align_bytes=64)
+        x_scales = x_mx.tile([P, IN_DIM], U8, align_bytes=64)
+        nc.vector.tensor_copy(out=write_regrouping(x_grouped[:]), in_=read_regrouping(x_rows[:]))
+        nc.vector.quantize_mx(
+            out=x_codes[:].bitcast(E4M3_X4),
+            scales=x_scales[:],
+            in_=x_grouped[:].rearrange("p c j -> p (c j)"),
+        )
+
+        def multiply_and_store(gate, half, d_grouped, vector_is_free):
+            d_codes = d_mx.tile([P, N_TILE], U32, align_bytes=64)
+            d_scales = d_mx.tile([P, N_TILE], U8, align_bytes=64)
+            nc.vector.quantize_mx(
+                out=d_codes[:].bitcast(E5M2_X4),
+                scales=d_scales[:],
+                in_=d_grouped[:].rearrange("p c j -> p (c j)"),
+            )
+            columns = slice(half * N_TILE, (half + 1) * N_TILE)
+            for first in range(0, M_TILES, M_TILES_PER_STORE):
+                staged = stage.tile([P, M_TILES_PER_STORE, N_TILE], F32)
+                for k in range(M_TILES_PER_STORE):
+                    x_columns = slice((first + k) * M_TILE, (first + k + 1) * M_TILE)
+                    bank = psum.tile([M_TILE, N_TILE], F32)
+                    nc.tensor.matmul_mx(
+                        out=bank[:],
+                        lhsT=x_codes[:, x_columns].bitcast(E4M3_X4),
+                        lhsT_scale=x_scales[:, x_columns],
+                        rhs=d_codes[:].bitcast(E5M2_X4),
+                        rhs_scale=d_scales[:],
+                        start=True,
+                        stop=True,
+                    )
+                    if vector_is_free and k % 2 == 1:
+                        nc.vector.tensor_copy(out=staged[:, k, :], in_=bank[:])
+                    else:
+                        nc.scalar.copy(out=staged[:, k, :], in_=bank[:])
+                nc.sync.dma_start(
+                    out=out_tiles[gate, :, first : first + M_TILES_PER_STORE, columns], in_=staged[:]
+                )
+
+        def new_d_grouped():
+            return d_mx.tile([P, N_TILE, PACK], BF16, name="d_grouped", align_bytes=64)
+
+        def half_of(rows_tile, half):
+            return rows_tile[:, :, half * N_TILE : (half + 1) * N_TILE]
+
+        g1z_neg = plane("g1z_neg")
+        gz1z_neg = plane("gz1z_neg")
+        for pair in TOKEN_PAIRS:
+            nc.vector.scalar_tensor_tensor(
+                out=g1z_neg[:, pair, :], in0=z[:, pair, :], scalar=1.0, in1=g_rows[:, pair, :],
+                op0=ALU.subtract, op1=ALU.mult,
+            )
+            nc.vector.tensor_tensor(
+                out=gz1z_neg[:, pair, :], in0=z[:, pair, :], in1=g1z_neg[:, pair, :], op=ALU.mult
+            )
+
+        n_squared = plane("n_squared")
+        dn = plane("dn")
+        for pair in TOKEN_PAIRS:
+            nc.scalar.activation(out=n_squared[:, pair, :], in_=n[:, pair, :], func=SQUARE)
+            nc.vector.scalar_tensor_tensor(
+                out=dn[:, pair, :], in0=n_squared[:, pair, :], scalar=1.0, in1=g1z_neg[:, pair, :],
+                op0=ALU.subtract, op1=ALU.mult,
+            )
+        for half in range(HALVES):
+            d_grouped = new_d_grouped()
+            nc.scalar.copy(out=write_regrouping(d_grouped[:]), in_=read_regrouping(half_of(dn, half)))
+            multiply_and_store(GATE_N, half, d_grouped, vector_is_free=False)
+
+        n_minus_hid = plane("n_minus_hid")
+        for pair in TOKEN_PAIRS:
+            nc.vector.tensor_tensor(
+                out=n_minus_hid[:, pair, :], in0=n[:, pair, :], in1=hid_rows[:, pair, :], op=ALU.subtract
+            )
+        for half in range(HALVES):
+            d_grouped = new_d_grouped()
+            nc.vector.tensor_tensor(
+                out=write_regrouping(d_grouped[:]),
+                in0=read_regrouping(half_of(n_minus_hid, half)),
+                in1=read_regrouping(half_of(gz1z_neg, half)),
+                op=ALU.mult,
+            )
+            multiply_and_store(GATE_Z, half, d_grouped, vector_is_free=False)
+
+        r1r_neg = plane("r1r_neg")
+        hn_r1r = plane("hn_r1r")
+        for pair in TOKEN_PAIRS:
+            nc.vector.scalar_tensor_tensor(
+                out=r1r_neg[:, pair, :], in0=r[:, pair, :], scalar=1.0, in1=r[:, pair, :],
+                op0=ALU.subtract, op1=ALU.mult,
+            )
+            nc.vector.scalar_tensor_tensor(
+                out=hn_r1r[:, pair, :], in0=hn_rows[:, pair, :], scalar=-1.0, in1=r1r_neg[:, pair, :],
+                op0=ALU.mult, op1=ALU.mult,
+            )
+        for half in range(HALVES):
+            d_grouped = new_d_grouped()
+            nc.vector.tensor_tensor(
+                out=write_regrouping(d_grouped[:]),
+                in0=read_regrouping(half_of(dn, half)),
+                in1=read_regrouping(half_of(hn_r1r, half)),
+                op=ALU.mult,
+            )
+            multiply_and_store(GATE_R, half, d_grouped, vector_is_free=(half == HALVES - 1))

@@ -24,14 +24,14 @@ M_TILE = P
 N_TILE = 512
 M_TILES = IN_DIM // M_TILE
 HALVES = HID_DIM // N_TILE
-M_TILES_PER_STORE = 4
+M_TILES_PER_STORE = 2
 
 TOKEN_PAIRS = (slice(0, 2), slice(2, 4))
 
 RUN = 4
 
-PLANE_SLOTS = 7
-STAGE_SLOTS = 6
+PLANE_SLOTS = 8
+STAGE_SLOTS = 8
 PSUM_BANKS = 8
 
 FLOPS = 2 * 3 * TOKENS * IN_DIM * HID_DIM
@@ -61,13 +61,10 @@ def tile_grucellv2_v_kernel(tc, x, hid, wx, wh, bx, bh, gates, hn, grad_out, out
         d_mx = ctx.enter_context(tc.tile_pool(name="d_mx", bufs=3))
         stage = ctx.enter_context(tc.tile_pool(name="stage", bufs=STAGE_SLOTS))
         psum = ctx.enter_context(tc.psum_pool(name="psum", bufs=PSUM_BANKS))
+        ctx.enter_context(tc.manual_schedule())
 
         def plane(name):
             return planes.tile([P, PACK, HID_DIM], F32, name=name, tag="plane")
-
-        def load(rows_tile, dram):
-            for pair in TOKEN_PAIRS:
-                nc.sync.dma_start(out=rows_tile[:, pair, :], in_=token_rows(dram)[:, pair, :])
 
         x_rows = narrow.tile([P, PACK, IN_DIM], BF16)
         g_rows = narrow.tile([P, PACK, HID_DIM], BF16)
@@ -81,10 +78,10 @@ def tile_grucellv2_v_kernel(tc, x, hid, wx, wh, bx, bh, gates, hn, grad_out, out
         for pair in TOKEN_PAIRS:
             nc.sync.dma_start(out=g_rows[:, pair, :], in_=token_rows(grad_out)[:, pair, :])
             nc.sync.dma_start(out=z[:, pair, :], in_=token_rows(gates[GATE_Z, :, :])[:, pair, :])
-        load(n, gates[GATE_N, :, :])
+            nc.sync.dma_start(out=n[:, pair, :], in_=token_rows(gates[GATE_N, :, :])[:, pair, :])
         nc.sync.dma_start(out=hid_rows[:], in_=token_rows(hid))
-        load(r, gates[GATE_R, :, :])
-        load(hn_rows, hn)
+        nc.sync.dma_start(out=r[:], in_=token_rows(gates[GATE_R, :, :]))
+        nc.sync.dma_start(out=hn_rows[:], in_=token_rows(hn))
 
         x_grouped = x_mx.tile([P, IN_DIM, PACK], BF16, align_bytes=64)
         x_codes = x_mx.tile([P, IN_DIM], U32, align_bytes=64)
@@ -135,33 +132,34 @@ def tile_grucellv2_v_kernel(tc, x, hid, wx, wh, bx, bh, gates, hn, grad_out, out
 
         g1z_neg = plane("g1z_neg")
         gz1z_neg = plane("gz1z_neg")
+        n_squared = plane("n_squared")
+        dn = plane("dn")
         for pair in TOKEN_PAIRS:
             nc.vector.scalar_tensor_tensor(
                 out=g1z_neg[:, pair, :], in0=z[:, pair, :], scalar=1.0, in1=g_rows[:, pair, :],
                 op0=ALU.subtract, op1=ALU.mult,
             )
+            nc.scalar.activation(out=n_squared[:, pair, :], in_=n[:, pair, :], func=SQUARE)
             nc.vector.tensor_tensor(
                 out=gz1z_neg[:, pair, :], in0=z[:, pair, :], in1=g1z_neg[:, pair, :], op=ALU.mult
             )
-
-        n_squared = plane("n_squared")
-        dn = plane("dn")
-        for pair in TOKEN_PAIRS:
-            nc.scalar.activation(out=n_squared[:, pair, :], in_=n[:, pair, :], func=SQUARE)
             nc.vector.scalar_tensor_tensor(
                 out=dn[:, pair, :], in0=n_squared[:, pair, :], scalar=1.0, in1=g1z_neg[:, pair, :],
                 op0=ALU.subtract, op1=ALU.mult,
             )
-        for half in range(HALVES):
-            d_grouped = new_d_grouped()
-            nc.scalar.copy(out=write_regrouping(d_grouped[:]), in_=read_regrouping(half_of(dn, half)))
-            multiply_and_store(GATE_N, half, d_grouped, vector_is_free=False)
 
+        dn_grouped = []
+        for half in range(HALVES):
+            dn_grouped.append(new_d_grouped())
+            nc.scalar.copy(out=write_regrouping(dn_grouped[half][:]), in_=read_regrouping(half_of(dn, half)))
         n_minus_hid = plane("n_minus_hid")
-        for pair in TOKEN_PAIRS:
+        for half in range(HALVES):
             nc.vector.tensor_tensor(
-                out=n_minus_hid[:, pair, :], in0=n[:, pair, :], in1=hid_rows[:, pair, :], op=ALU.subtract
+                out=half_of(n_minus_hid, half), in0=half_of(n, half), in1=half_of(hid_rows, half),
+                op=ALU.subtract,
             )
+            multiply_and_store(GATE_N, half, dn_grouped[half], vector_is_free=False)
+
         for half in range(HALVES):
             d_grouped = new_d_grouped()
             nc.vector.tensor_tensor(
@@ -174,16 +172,15 @@ def tile_grucellv2_v_kernel(tc, x, hid, wx, wh, bx, bh, gates, hn, grad_out, out
 
         r1r_neg = plane("r1r_neg")
         hn_r1r = plane("hn_r1r")
-        for pair in TOKEN_PAIRS:
+        for half in range(HALVES):
             nc.vector.scalar_tensor_tensor(
-                out=r1r_neg[:, pair, :], in0=r[:, pair, :], scalar=1.0, in1=r[:, pair, :],
+                out=half_of(r1r_neg, half), in0=half_of(r, half), scalar=1.0, in1=half_of(r, half),
                 op0=ALU.subtract, op1=ALU.mult,
             )
             nc.vector.scalar_tensor_tensor(
-                out=hn_r1r[:, pair, :], in0=hn_rows[:, pair, :], scalar=-1.0, in1=r1r_neg[:, pair, :],
+                out=half_of(hn_r1r, half), in0=half_of(hn_rows, half), scalar=-1.0, in1=half_of(r1r_neg, half),
                 op0=ALU.mult, op1=ALU.mult,
             )
-        for half in range(HALVES):
             d_grouped = new_d_grouped()
             nc.vector.tensor_tensor(
                 out=write_regrouping(d_grouped[:]),

@@ -26,11 +26,14 @@ M_TILES = IN_DIM // M_TILE
 HALVES = HID_DIM // N_TILE
 M_TILES_PER_STORE = 2
 
-TOKEN_PAIRS = (slice(0, 2), slice(2, 4))
+TOKEN_PAIRS = ((0, 1), (2, 3))
+
+PIECE = N_TILE // 2
+PIECES_PER_HALF = N_TILE // PIECE
 
 RUN = 4
 
-PLANE_SLOTS = 8
+PLANE_SLOTS = 7
 STAGE_SLOTS = 8
 PSUM_BANKS = 8
 
@@ -66,6 +69,10 @@ def tile_grucellv2_v_kernel(tc, x, hid, wx, wh, bx, bh, gates, hn, grad_out, out
         def plane(name):
             return planes.tile([P, PACK, HID_DIM], F32, name=name, tag="plane")
 
+        def load_pair(rows_tile, dram, pair):
+            rows = slice(pair[0], pair[-1] + 1)
+            nc.sync.dma_start(out=rows_tile[:, rows, :], in_=token_rows(dram)[:, rows, :])
+
         x_rows = narrow.tile([P, PACK, IN_DIM], BF16)
         g_rows = narrow.tile([P, PACK, HID_DIM], BF16)
         hid_rows = narrow.tile([P, PACK, HID_DIM], BF16)
@@ -74,33 +81,39 @@ def tile_grucellv2_v_kernel(tc, x, hid, wx, wh, bx, bh, gates, hn, grad_out, out
         r = plane("r")
         hn_rows = plane("hn_rows")
 
-        nc.sync.dma_start(out=x_rows[:], in_=token_rows(x))
         for pair in TOKEN_PAIRS:
-            nc.sync.dma_start(out=g_rows[:, pair, :], in_=token_rows(grad_out)[:, pair, :])
-            nc.sync.dma_start(out=z[:, pair, :], in_=token_rows(gates[GATE_Z, :, :])[:, pair, :])
-            nc.sync.dma_start(out=n[:, pair, :], in_=token_rows(gates[GATE_N, :, :])[:, pair, :])
+            load_pair(g_rows, grad_out, pair)
+            load_pair(z, gates[GATE_Z, :, :], pair)
+        for pair in TOKEN_PAIRS:
+            load_pair(n, gates[GATE_N, :, :], pair)
+        nc.sync.dma_start(out=x_rows[:], in_=token_rows(x))
         nc.sync.dma_start(out=hid_rows[:], in_=token_rows(hid))
         nc.sync.dma_start(out=r[:], in_=token_rows(gates[GATE_R, :, :]))
         nc.sync.dma_start(out=hn_rows[:], in_=token_rows(hn))
 
-        x_grouped = x_mx.tile([P, IN_DIM, PACK], BF16, align_bytes=64)
-        x_codes = x_mx.tile([P, IN_DIM], U32, align_bytes=64)
-        x_scales = x_mx.tile([P, IN_DIM], U8, align_bytes=64)
-        nc.vector.tensor_copy(out=write_regrouping(x_grouped[:]), in_=read_regrouping(x_rows[:]))
-        nc.vector.quantize_mx(
-            out=x_codes[:].bitcast(E4M3_X4),
-            scales=x_scales[:],
-            in_=x_grouped[:].rearrange("p c j -> p (c j)"),
-        )
+        def new_d_grouped():
+            return d_mx.tile([P, N_TILE, PACK], BF16, name="d_grouped", align_bytes=64)
+
+        def half_of(rows_tile, half):
+            return rows_tile[:, :, half * N_TILE : (half + 1) * N_TILE]
+
+        def piece_of(rows_tile, half, k):
+            start = half * N_TILE + k * PIECE
+            return rows_tile[:, :, start : start + PIECE]
+
+        def grouped_piece(d_grouped, k):
+            return d_grouped[:, k * PIECE : (k + 1) * PIECE, :]
 
         def multiply_and_store(gate, half, d_grouped, vector_is_free):
             d_codes = d_mx.tile([P, N_TILE], U32, align_bytes=64)
             d_scales = d_mx.tile([P, N_TILE], U8, align_bytes=64)
-            nc.vector.quantize_mx(
-                out=d_codes[:].bitcast(E5M2_X4),
-                scales=d_scales[:],
-                in_=d_grouped[:].rearrange("p c j -> p (c j)"),
-            )
+            for k in range(PIECES_PER_HALF):
+                piece = slice(k * PIECE, (k + 1) * PIECE)
+                nc.vector.quantize_mx(
+                    out=d_codes[:, piece].bitcast(E5M2_X4),
+                    scales=d_scales[:, piece],
+                    in_=grouped_piece(d_grouped, k).rearrange("p c j -> p (c j)"),
+                )
             columns = slice(half * N_TILE, (half + 1) * N_TILE)
             for first in range(0, M_TILES, M_TILES_PER_STORE):
                 staged = stage.tile([P, M_TILES_PER_STORE, N_TILE], F32)
@@ -124,30 +137,29 @@ def tile_grucellv2_v_kernel(tc, x, hid, wx, wh, bx, bh, gates, hn, grad_out, out
                     out=out_tiles[gate, :, first : first + M_TILES_PER_STORE, columns], in_=staged[:]
                 )
 
-        def new_d_grouped():
-            return d_mx.tile([P, N_TILE, PACK], BF16, name="d_grouped", align_bytes=64)
-
-        def half_of(rows_tile, half):
-            return rows_tile[:, :, half * N_TILE : (half + 1) * N_TILE]
-
         g1z_neg = plane("g1z_neg")
         gz1z_neg = plane("gz1z_neg")
+        for pair in TOKEN_PAIRS:
+            for j in pair:
+                nc.vector.scalar_tensor_tensor(
+                    out=g1z_neg[:, j, :], in0=z[:, j, :], scalar=1.0, in1=g_rows[:, j, :],
+                    op0=ALU.subtract, op1=ALU.mult,
+                )
+            for j in pair:
+                nc.vector.tensor_tensor(out=gz1z_neg[:, j, :], in0=z[:, j, :], in1=g1z_neg[:, j, :], op=ALU.mult)
+
         n_squared = plane("n_squared")
         dn = plane("dn")
         for pair in TOKEN_PAIRS:
+            rows = slice(pair[0], pair[-1] + 1)
+            nc.scalar.activation(out=n_squared[:, rows, :], in_=n[:, rows, :], func=SQUARE)
             nc.vector.scalar_tensor_tensor(
-                out=g1z_neg[:, pair, :], in0=z[:, pair, :], scalar=1.0, in1=g_rows[:, pair, :],
-                op0=ALU.subtract, op1=ALU.mult,
-            )
-            nc.scalar.activation(out=n_squared[:, pair, :], in_=n[:, pair, :], func=SQUARE)
-            nc.vector.tensor_tensor(
-                out=gz1z_neg[:, pair, :], in0=z[:, pair, :], in1=g1z_neg[:, pair, :], op=ALU.mult
-            )
-            nc.vector.scalar_tensor_tensor(
-                out=dn[:, pair, :], in0=n_squared[:, pair, :], scalar=1.0, in1=g1z_neg[:, pair, :],
+                out=dn[:, rows, :], in0=n_squared[:, rows, :], scalar=1.0, in1=g1z_neg[:, rows, :],
                 op0=ALU.subtract, op1=ALU.mult,
             )
 
+        x_grouped = x_mx.tile([P, IN_DIM, PACK], BF16, align_bytes=64)
+        nc.scalar.copy(out=write_regrouping(x_grouped[:]), in_=read_regrouping(x_rows[:]))
         dn_grouped = []
         for half in range(HALVES):
             dn_grouped.append(new_d_grouped())
@@ -158,34 +170,48 @@ def tile_grucellv2_v_kernel(tc, x, hid, wx, wh, bx, bh, gates, hn, grad_out, out
                 out=half_of(n_minus_hid, half), in0=half_of(n, half), in1=half_of(hid_rows, half),
                 op=ALU.subtract,
             )
+
+        x_codes = x_mx.tile([P, IN_DIM], U32, align_bytes=64)
+        x_scales = x_mx.tile([P, IN_DIM], U8, align_bytes=64)
+        nc.vector.quantize_mx(
+            out=x_codes[:].bitcast(E4M3_X4),
+            scales=x_scales[:],
+            in_=x_grouped[:].rearrange("p c j -> p (c j)"),
+        )
+
+        for half in range(HALVES):
             multiply_and_store(GATE_N, half, dn_grouped[half], vector_is_free=False)
 
         for half in range(HALVES):
             d_grouped = new_d_grouped()
-            nc.vector.tensor_tensor(
-                out=write_regrouping(d_grouped[:]),
-                in0=read_regrouping(half_of(n_minus_hid, half)),
-                in1=read_regrouping(half_of(gz1z_neg, half)),
-                op=ALU.mult,
-            )
+            for k in range(PIECES_PER_HALF):
+                nc.vector.tensor_tensor(
+                    out=write_regrouping(grouped_piece(d_grouped, k)),
+                    in0=read_regrouping(piece_of(n_minus_hid, half, k)),
+                    in1=read_regrouping(piece_of(gz1z_neg, half, k)),
+                    op=ALU.mult,
+                )
             multiply_and_store(GATE_Z, half, d_grouped, vector_is_free=False)
 
         r1r_neg = plane("r1r_neg")
         hn_r1r = plane("hn_r1r")
         for half in range(HALVES):
-            nc.vector.scalar_tensor_tensor(
-                out=half_of(r1r_neg, half), in0=half_of(r, half), scalar=1.0, in1=half_of(r, half),
-                op0=ALU.subtract, op1=ALU.mult,
-            )
-            nc.vector.scalar_tensor_tensor(
-                out=half_of(hn_r1r, half), in0=half_of(hn_rows, half), scalar=-1.0, in1=half_of(r1r_neg, half),
-                op0=ALU.mult, op1=ALU.mult,
-            )
+            for k in range(PIECES_PER_HALF):
+                nc.vector.scalar_tensor_tensor(
+                    out=piece_of(r1r_neg, half, k), in0=piece_of(r, half, k), scalar=1.0, in1=piece_of(r, half, k),
+                    op0=ALU.subtract, op1=ALU.mult,
+                )
+            for k in range(PIECES_PER_HALF):
+                nc.vector.scalar_tensor_tensor(
+                    out=piece_of(hn_r1r, half, k), in0=piece_of(hn_rows, half, k), scalar=-1.0,
+                    in1=piece_of(r1r_neg, half, k), op0=ALU.mult, op1=ALU.mult,
+                )
             d_grouped = new_d_grouped()
-            nc.vector.tensor_tensor(
-                out=write_regrouping(d_grouped[:]),
-                in0=read_regrouping(half_of(dn, half)),
-                in1=read_regrouping(half_of(hn_r1r, half)),
-                op=ALU.mult,
-            )
+            for k in range(PIECES_PER_HALF):
+                nc.vector.tensor_tensor(
+                    out=write_regrouping(grouped_piece(d_grouped, k)),
+                    in0=read_regrouping(piece_of(dn, half, k)),
+                    in1=read_regrouping(piece_of(hn_r1r, half, k)),
+                    op=ALU.mult,
+                )
             multiply_and_store(GATE_R, half, d_grouped, vector_is_free=(half == HALVES - 1))

@@ -24,7 +24,7 @@ M_TILE = P
 N_TILE = 512
 M_TILES = IN_DIM // M_TILE
 HALVES = HID_DIM // N_TILE
-M_TILES_PER_STORE = 2
+STORE_WIDTH = 2 * N_TILE
 
 TOKEN_PAIRS = ((0, 1), (2, 3))
 
@@ -34,6 +34,7 @@ PIECES_PER_HALF = N_TILE // PIECE
 RUN = 4
 
 PLANE_SLOTS = 7
+D_SLOTS = 4
 STAGE_SLOTS = 8
 PSUM_BANKS = 8
 
@@ -61,7 +62,7 @@ def tile_grucellv2_v_kernel(tc, x, hid, wx, wh, bx, bh, gates, hn, grad_out, out
         narrow = ctx.enter_context(tc.tile_pool(name="narrow", bufs=1))
         planes = ctx.enter_context(tc.tile_pool(name="planes", bufs=PLANE_SLOTS))
         x_mx = ctx.enter_context(tc.tile_pool(name="x_mx", bufs=1))
-        d_mx = ctx.enter_context(tc.tile_pool(name="d_mx", bufs=3))
+        d_mx = ctx.enter_context(tc.tile_pool(name="d_mx", bufs=D_SLOTS))
         stage = ctx.enter_context(tc.tile_pool(name="stage", bufs=STAGE_SLOTS))
         psum = ctx.enter_context(tc.psum_pool(name="psum", bufs=PSUM_BANKS))
         ctx.enter_context(tc.manual_schedule())
@@ -104,7 +105,7 @@ def tile_grucellv2_v_kernel(tc, x, hid, wx, wh, bx, bh, gates, hn, grad_out, out
         def grouped_piece(d_grouped, k):
             return d_grouped[:, k * PIECE : (k + 1) * PIECE, :]
 
-        def multiply_and_store(gate, half, d_grouped, vector_is_free):
+        def quantise(d_grouped):
             d_codes = d_mx.tile([P, N_TILE], U32, align_bytes=64)
             d_scales = d_mx.tile([P, N_TILE], U8, align_bytes=64)
             for k in range(PIECES_PER_HALF):
@@ -114,28 +115,33 @@ def tile_grucellv2_v_kernel(tc, x, hid, wx, wh, bx, bh, gates, hn, grad_out, out
                     scales=d_scales[:, piece],
                     in_=grouped_piece(d_grouped, k).rearrange("p c j -> p (c j)"),
                 )
-            columns = slice(half * N_TILE, (half + 1) * N_TILE)
-            for first in range(0, M_TILES, M_TILES_PER_STORE):
-                staged = stage.tile([P, M_TILES_PER_STORE, N_TILE], F32)
-                for k in range(M_TILES_PER_STORE):
+            return d_codes, d_scales
+
+        def multiply_and_store(gate, first_half, operands, vector_is_free):
+            width = len(operands) * N_TILE
+            columns = slice(first_half * N_TILE, first_half * N_TILE + width)
+            tiles_per_store = STORE_WIDTH // width
+            for first in range(0, M_TILES, tiles_per_store):
+                staged = stage.tile([P, tiles_per_store, width], F32)
+                for k in range(tiles_per_store):
                     x_columns = slice((first + k) * M_TILE, (first + k + 1) * M_TILE)
-                    bank = psum.tile([M_TILE, N_TILE], F32)
-                    nc.tensor.matmul_mx(
-                        out=bank[:],
-                        lhsT=x_codes[:, x_columns].bitcast(E4M3_X4),
-                        lhsT_scale=x_scales[:, x_columns],
-                        rhs=d_codes[:].bitcast(E5M2_X4),
-                        rhs_scale=d_scales[:],
-                        start=True,
-                        stop=True,
-                    )
-                    if vector_is_free and k % 2 == 1:
-                        nc.vector.tensor_copy(out=staged[:, k, :], in_=bank[:])
-                    else:
-                        nc.scalar.copy(out=staged[:, k, :], in_=bank[:])
-                nc.sync.dma_start(
-                    out=out_tiles[gate, :, first : first + M_TILES_PER_STORE, columns], in_=staged[:]
-                )
+                    for h, (d_codes, d_scales) in enumerate(operands):
+                        bank = psum.tile([M_TILE, N_TILE], F32)
+                        nc.tensor.matmul_mx(
+                            out=bank[:],
+                            lhsT=x_codes[:, x_columns].bitcast(E4M3_X4),
+                            lhsT_scale=x_scales[:, x_columns],
+                            rhs=d_codes[:].bitcast(E5M2_X4),
+                            rhs_scale=d_scales[:],
+                            start=True,
+                            stop=True,
+                        )
+                        place = staged[:, k, h * N_TILE : (h + 1) * N_TILE]
+                        if vector_is_free and k + h == 1:
+                            nc.vector.tensor_copy(out=place, in_=bank[:])
+                        else:
+                            nc.scalar.copy(out=place, in_=bank[:])
+                nc.sync.dma_start(out=out_tiles[gate, :, first : first + tiles_per_store, columns], in_=staged[:])
 
         g1z_neg = plane("g1z_neg")
         gz1z_neg = plane("gz1z_neg")
@@ -179,19 +185,18 @@ def tile_grucellv2_v_kernel(tc, x, hid, wx, wh, bx, bh, gates, hn, grad_out, out
             in_=x_grouped[:].rearrange("p c j -> p (c j)"),
         )
 
-        for half in range(HALVES):
-            multiply_and_store(GATE_N, half, dn_grouped[half], vector_is_free=False)
+        multiply_and_store(GATE_N, 0, [quantise(d_grouped) for d_grouped in dn_grouped], vector_is_free=False)
 
+        dz_grouped = []
         for half in range(HALVES):
-            d_grouped = new_d_grouped()
-            for k in range(PIECES_PER_HALF):
-                nc.vector.tensor_tensor(
-                    out=write_regrouping(grouped_piece(d_grouped, k)),
-                    in0=read_regrouping(piece_of(n_minus_hid, half, k)),
-                    in1=read_regrouping(piece_of(gz1z_neg, half, k)),
-                    op=ALU.mult,
-                )
-            multiply_and_store(GATE_Z, half, d_grouped, vector_is_free=False)
+            dz_grouped.append(new_d_grouped())
+            nc.vector.tensor_tensor(
+                out=write_regrouping(dz_grouped[half][:]),
+                in0=read_regrouping(half_of(n_minus_hid, half)),
+                in1=read_regrouping(half_of(gz1z_neg, half)),
+                op=ALU.mult,
+            )
+        multiply_and_store(GATE_Z, 0, [quantise(d_grouped) for d_grouped in dz_grouped], vector_is_free=False)
 
         r1r_neg = plane("r1r_neg")
         hn_r1r = plane("hn_r1r")
@@ -214,4 +219,4 @@ def tile_grucellv2_v_kernel(tc, x, hid, wx, wh, bx, bh, gates, hn, grad_out, out
                     in1=read_regrouping(piece_of(hn_r1r, half, k)),
                     op=ALU.mult,
                 )
-            multiply_and_store(GATE_R, half, d_grouped, vector_is_free=(half == HALVES - 1))
+            multiply_and_store(GATE_R, half, [quantise(d_grouped)], vector_is_free=(half == HALVES - 1))

@@ -1,6 +1,7 @@
 from contextlib import ExitStack
 
 import concourse.mybir as mybir
+from concourse.masks import make_identity
 
 F32 = mybir.dt.float32
 BF16 = mybir.dt.bfloat16
@@ -9,7 +10,7 @@ U8 = mybir.dt.uint8
 E4M3_X4 = mybir.dt.float8_e4m3fn_x4
 E5M2_X4 = mybir.dt.float8_e5m2_x4
 ALU = mybir.AluOpType
-SQUARE = mybir.ActivationFunctionType.Square
+ACT = mybir.ActivationFunctionType
 
 P = 128
 PACK = 4
@@ -19,24 +20,21 @@ HID_DIM = 1024
 GATE_R = 0
 GATE_Z = 1
 GATE_N = 2
-
 M_TILE = P
-N_TILE = 512
 M_TILES = IN_DIM // M_TILE
+N_TILE = 512
 HALVES = HID_DIM // N_TILE
-STORE_WIDTH = 2 * N_TILE
-
-TOKEN_PAIRS = ((0, 1), (2, 3))
-
-PIECE = N_TILE // 2
-PIECES_PER_HALF = N_TILE // PIECE
-
+BLOCKS = 2
+TILES_PER_BLOCK = 4
+BLOCK_WIDTH = IN_DIM // BLOCKS
 RUN = 4
-
-PLANE_SLOTS = 7
-D_SLOTS = 4
-STAGE_SLOTS = 8
-PSUM_BANKS = 8
+EIGHTH = 128
+EIGHTHS = HID_DIM // EIGHTH
+N_PE = 6
+QUARTER = 256
+QUARTERS = HID_DIM // QUARTER
+STAGE_SLOTS = 5
+V_LAST = 8
 
 FLOPS = 2 * 3 * TOKENS * IN_DIM * HID_DIM
 BYTES = 3 * TOKENS * 1024 * 2 + 4 * TOKENS * 1024 * 4 + 3 * IN_DIM * HID_DIM * 4
@@ -56,167 +54,178 @@ def write_regrouping(grouped):
 
 def tile_grucellv2_v_kernel(tc, x, hid, wx, wh, bx, bh, gates, hn, grad_out, out):
     nc = tc.nc
-    out_tiles = out.rearrange("g (t m) h -> g m t h", m=M_TILE)
+    out_blocks = out.rearrange("g (b m t) h -> g m b t h", b=BLOCKS, t=TILES_PER_BLOCK)
 
     with ExitStack() as ctx:
-        narrow = ctx.enter_context(tc.tile_pool(name="narrow", bufs=1))
-        planes = ctx.enter_context(tc.tile_pool(name="planes", bufs=PLANE_SLOTS))
-        x_mx = ctx.enter_context(tc.tile_pool(name="x_mx", bufs=1))
-        d_mx = ctx.enter_context(tc.tile_pool(name="d_mx", bufs=D_SLOTS))
+        keep = ctx.enter_context(tc.tile_pool(name="keep", bufs=1))
+        d_pool = ctx.enter_context(tc.tile_pool(name="d_pool", bufs=2))
         stage = ctx.enter_context(tc.tile_pool(name="stage", bufs=STAGE_SLOTS))
-        psum = ctx.enter_context(tc.psum_pool(name="psum", bufs=PSUM_BANKS))
+        psum_few = ctx.enter_context(tc.psum_pool(name="psum_few", bufs=8 - N_PE))
+        psum_many = ctx.enter_context(tc.psum_pool(name="psum_many", bufs=N_PE))
         ctx.enter_context(tc.manual_schedule())
 
-        def plane(name):
-            return planes.tile([P, PACK, HID_DIM], F32, name=name, tag="plane")
+        x_rows = keep.tile([P, PACK, IN_DIM], BF16)
+        g_rows = keep.tile([P, PACK, HID_DIM], BF16)
+        hid_rows = keep.tile([P, PACK, HID_DIM], BF16)
+        z = keep.tile([P, PACK, HID_DIM], F32)
+        n = keep.tile([P, PACK, HID_DIM], F32)
+        r = keep.tile([P, PACK, HID_DIM], F32)
+        hn_rows = keep.tile([P, PACK, HID_DIM], F32)
 
-        def load_pair(rows_tile, dram, pair):
-            rows = slice(pair[0], pair[-1] + 1)
-            nc.sync.dma_start(out=rows_tile[:, rows, :], in_=token_rows(dram)[:, rows, :])
+        def load(rows_tile, dram, first, last):
+            nc.sync.dma_start(out=rows_tile[:, first:last, :], in_=token_rows(dram)[:, first:last, :])
 
-        x_rows = narrow.tile([P, PACK, IN_DIM], BF16)
-        g_rows = narrow.tile([P, PACK, HID_DIM], BF16)
-        hid_rows = narrow.tile([P, PACK, HID_DIM], BF16)
-        z = plane("z")
-        n = plane("n")
-        r = plane("r")
-        hn_rows = plane("hn_rows")
+        for first, last in ((0, 1), (1, 2), (2, 4)):
+            load(g_rows, grad_out, first, last)
+            load(z, gates[GATE_Z, :, :], first, last)
+        for j in range(PACK):
+            load(n, gates[GATE_N, :, :], j, j + 1)
+        load(x_rows, x, 0, PACK)
+        load(hid_rows, hid, 0, PACK)
+        load(r, gates[GATE_R, :, :], 0, PACK)
+        load(hn_rows, hn, 0, PACK)
 
-        for pair in TOKEN_PAIRS:
-            load_pair(g_rows, grad_out, pair)
-            load_pair(z, gates[GATE_Z, :, :], pair)
-        for pair in TOKEN_PAIRS:
-            load_pair(n, gates[GATE_N, :, :], pair)
-        nc.sync.dma_start(out=x_rows[:], in_=token_rows(x))
-        nc.sync.dma_start(out=hid_rows[:], in_=token_rows(hid))
-        nc.sync.dma_start(out=r[:], in_=token_rows(gates[GATE_R, :, :]))
-        nc.sync.dma_start(out=hn_rows[:], in_=token_rows(hn))
+        ident = keep.tile([P, P], F32)
+        make_identity(nc, ident[:])
+        neg_ident = keep.tile([P, P], BF16)
+        nc.gpsimd.tensor_scalar(out=neg_ident[:], in0=ident[:], scalar1=-1.0, scalar2=0.0, op0=ALU.mult, op1=ALU.add)
 
-        def new_d_grouped():
-            return d_mx.tile([P, N_TILE, PACK], BF16, name="d_grouped", align_bytes=64)
+        a_neg = keep.tile([P, PACK, HID_DIM], F32)
+        gz_neg = keep.tile([P, PACK, HID_DIM], F32)
+        dn = keep.tile([P, PACK, HID_DIM], F32)
 
-        def half_of(rows_tile, half):
-            return rows_tile[:, :, half * N_TILE : (half + 1) * N_TILE]
+        def make_a(j):
+            nc.vector.scalar_tensor_tensor(out=a_neg[:, j, :], in0=z[:, j, :], scalar=1.0, in1=g_rows[:, j, :],
+                                           op0=ALU.subtract, op1=ALU.mult)
 
-        def piece_of(rows_tile, half, k):
-            start = half * N_TILE + k * PIECE
-            return rows_tile[:, :, start : start + PIECE]
+        def make_gz(j):
+            nc.vector.tensor_tensor(out=gz_neg[:, j, :], in0=z[:, j, :], in1=a_neg[:, j, :], op=ALU.mult)
 
-        def grouped_piece(d_grouped, k):
-            return d_grouped[:, k * PIECE : (k + 1) * PIECE, :]
+        def make_dn(j):
+            nc.scalar.activation(out=dn[:, j, :], in_=n[:, j, :], func=ACT.Square)
+            nc.vector.scalar_tensor_tensor(out=dn[:, j, :], in0=dn[:, j, :], scalar=1.0, in1=a_neg[:, j, :],
+                                           op0=ALU.subtract, op1=ALU.mult)
 
-        def quantise(d_grouped):
-            d_codes = d_mx.tile([P, N_TILE], U32, align_bytes=64)
-            d_scales = d_mx.tile([P, N_TILE], U8, align_bytes=64)
-            for k in range(PIECES_PER_HALF):
-                piece = slice(k * PIECE, (k + 1) * PIECE)
-                nc.vector.quantize_mx(
-                    out=d_codes[:, piece].bitcast(E5M2_X4),
-                    scales=d_scales[:, piece],
-                    in_=grouped_piece(d_grouped, k).rearrange("p c j -> p (c j)"),
-                )
-            return d_codes, d_scales
+        make_a(0)
+        make_a(1)
+        make_gz(0)
+        make_gz(1)
+        make_a(2)
+        make_a(3)
+        for j in range(PACK):
+            make_dn(j)
 
-        def multiply_and_store(gate, first_half, operands, vector_is_free):
-            width = len(operands) * N_TILE
-            columns = slice(first_half * N_TILE, first_half * N_TILE + width)
-            tiles_per_store = STORE_WIDTH // width
-            for first in range(0, M_TILES, tiles_per_store):
-                staged = stage.tile([P, tiles_per_store, width], F32)
-                for k in range(tiles_per_store):
-                    x_columns = slice((first + k) * M_TILE, (first + k + 1) * M_TILE)
-                    for h, (d_codes, d_scales) in enumerate(operands):
-                        bank = psum.tile([M_TILE, N_TILE], F32)
-                        nc.tensor.matmul_mx(
-                            out=bank[:],
-                            lhsT=x_codes[:, x_columns].bitcast(E4M3_X4),
-                            lhsT_scale=x_scales[:, x_columns],
-                            rhs=d_codes[:].bitcast(E5M2_X4),
-                            rhs_scale=d_scales[:],
-                            start=True,
-                            stop=True,
-                        )
-                        place = staged[:, k, h * N_TILE : (h + 1) * N_TILE]
-                        if vector_is_free and k + h == 1:
+        def eighth(rows_tile, e):
+            return rows_tile[:, :, e * EIGHTH:(e + 1) * EIGHTH]
+
+        nmh = []
+        for e in range(N_PE):
+            bank = psum_many.tile([P, PACK, EIGHTH], F32, name="bank")
+            nmh.append(bank)
+            nc.tensor.matmul(out=bank[:], lhsT=ident[:], rhs=eighth(n, e), start=True, stop=False)
+        for e in range(N_PE):
+            nc.tensor.matmul(out=nmh[e][:], lhsT=neg_ident[:], rhs=eighth(hid_rows, e), start=False, stop=True)
+
+        x_grouped = keep.tile([P, IN_DIM, PACK], BF16, align_bytes=64)
+        x_codes = keep.tile([P, IN_DIM], U32, align_bytes=64)
+        x_scales = keep.tile([P, IN_DIM], U8, align_bytes=64)
+        for b in range(BLOCKS):
+            cols = slice(b * BLOCK_WIDTH, (b + 1) * BLOCK_WIDTH)
+            nc.vector.tensor_copy(out=x_grouped[:, cols, :].rearrange("p (t m) j -> p m j t", t=TILES_PER_BLOCK),
+                                  in_=x_rows[:, :, cols].rearrange("p j (m t) -> p m j t", t=TILES_PER_BLOCK))
+        for b in range(BLOCKS):
+            cols = slice(b * BLOCK_WIDTH, (b + 1) * BLOCK_WIDTH)
+            nc.vector.quantize_mx(out=x_codes[:, cols].bitcast(E4M3_X4), scales=x_scales[:, cols],
+                                  in_=x_grouped[:, cols, :].rearrange("p c j -> p (c j)"))
+
+        def d_tiles(name):
+            grouped = d_pool.tile([P, HID_DIM, PACK], BF16, name="grouped", align_bytes=64)
+            codes = keep.tile([P, HID_DIM], U32, name="codes_" + name, align_bytes=64)
+            scales = keep.tile([P, HID_DIM], U8, name="scales_" + name, align_bytes=64)
+            return grouped, codes, scales
+
+        def quantise(d, c):
+            grouped, codes, scales = d
+            cols = slice(c * QUARTER, (c + 1) * QUARTER)
+            nc.vector.quantize_mx(out=codes[:, cols].bitcast(E5M2_X4), scales=scales[:, cols],
+                                  in_=grouped[:, cols, :].rearrange("p c j -> p (c j)"))
+
+        d_n = d_tiles("n")
+        for half in range(HALVES):
+            cols = slice(half * N_TILE, (half + 1) * N_TILE)
+            nc.scalar.copy(out=write_regrouping(d_n[0][:, cols, :]), in_=read_regrouping(dn[:, :, cols]))
+        quantise(d_n, 0)
+        quantise(d_n, 1)
+        make_gz(2)
+        quantise(d_n, 2)
+        quantise(d_n, 3)
+        make_gz(3)
+
+        def multiply_and_store(gate, d, halves, groups, many_banks, vector_last=0):
+            width = len(halves) * N_TILE
+            columns = slice(halves[0] * N_TILE, halves[0] * N_TILE + width)
+            idx = 0
+            count = 0
+            total = M_TILES * len(halves)
+            for size in groups:
+                staged = stage.tile([P, size, width], F32, name="staged")
+                for k in range(size):
+                    xc = slice(idx * M_TILE, (idx + 1) * M_TILE)
+                    for h, half in enumerate(halves):
+                        if many_banks and count % 8 < N_PE:
+                            bank = psum_many.tile([P, N_TILE], F32, name="bank")
+                        else:
+                            bank = psum_few.tile([P, N_TILE], F32, name="bank")
+                        dc = slice(half * N_TILE, (half + 1) * N_TILE)
+                        nc.tensor.matmul_mx(out=bank[:], lhsT=x_codes[:, xc].bitcast(E4M3_X4), lhsT_scale=x_scales[:, xc],
+                                            rhs=d[1][:, dc].bitcast(E5M2_X4), rhs_scale=d[2][:, dc], start=True, stop=True)
+                        place = staged[:, k, h * N_TILE:(h + 1) * N_TILE]
+                        if count >= total - vector_last and count % 2 == 1:
                             nc.vector.tensor_copy(out=place, in_=bank[:])
                         else:
                             nc.scalar.copy(out=place, in_=bank[:])
-                nc.sync.dma_start(out=out_tiles[gate, :, first : first + tiles_per_store, columns], in_=staged[:])
+                        count += 1
+                    idx += 1
+                first = idx - size
+                b, t = first // TILES_PER_BLOCK, first % TILES_PER_BLOCK
+                nc.sync.dma_start(out=out_blocks[gate, :, b, t:t + size, columns], in_=staged[:])
 
-        g1z_neg = plane("g1z_neg")
-        gz1z_neg = plane("gz1z_neg")
-        for pair in TOKEN_PAIRS:
-            for j in pair:
-                nc.vector.scalar_tensor_tensor(
-                    out=g1z_neg[:, j, :], in0=z[:, j, :], scalar=1.0, in1=g_rows[:, j, :],
-                    op0=ALU.subtract, op1=ALU.mult,
-                )
-            for j in pair:
-                nc.vector.tensor_tensor(out=gz1z_neg[:, j, :], in0=z[:, j, :], in1=g1z_neg[:, j, :], op=ALU.mult)
+        multiply_and_store(GATE_N, d_n, (0, 1), (1, 1, 2, 2, 2), many_banks=False)
 
-        n_squared = plane("n_squared")
-        dn = plane("dn")
-        for pair in TOKEN_PAIRS:
-            rows = slice(pair[0], pair[-1] + 1)
-            nc.scalar.activation(out=n_squared[:, rows, :], in_=n[:, rows, :], func=SQUARE)
-            nc.vector.scalar_tensor_tensor(
-                out=dn[:, rows, :], in0=n_squared[:, rows, :], scalar=1.0, in1=g1z_neg[:, rows, :],
-                op0=ALU.subtract, op1=ALU.mult,
-            )
+        d_z = d_tiles("z")
+        nmh_v = keep.tile([P, PACK, (EIGHTHS - N_PE) * EIGHTH], F32)
+        rest = slice(N_PE * EIGHTH, HID_DIM)
+        nc.vector.tensor_tensor(out=nmh_v[:], in0=n[:, :, rest], in1=hid_rows[:, :, rest], op=ALU.subtract)
+        for e in range(N_PE):
+            cols = slice(e * EIGHTH, (e + 1) * EIGHTH)
+            nc.vector.tensor_tensor(out=write_regrouping(d_z[0][:, cols, :]), in0=read_regrouping(gz_neg[:, :, cols]),
+                                    in1=read_regrouping(nmh[e][:]), op=ALU.mult)
+        nc.vector.tensor_tensor(out=write_regrouping(d_z[0][:, rest, :]), in0=read_regrouping(gz_neg[:, :, rest]),
+                                in1=read_regrouping(nmh_v[:]), op=ALU.mult)
+        for c in range(QUARTERS):
+            quantise(d_z, c)
+        multiply_and_store(GATE_Z, d_z, (0, 1), (2, 2, 2, 2), many_banks=True)
 
-        x_grouped = x_mx.tile([P, IN_DIM, PACK], BF16, align_bytes=64)
-        nc.scalar.copy(out=write_regrouping(x_grouped[:]), in_=read_regrouping(x_rows[:]))
-        dn_grouped = []
+        d_r = d_tiles("r")
+        r1r_neg = z
+        hn_r1r = a_neg
+
+        def quarter(rows_tile, c):
+            return rows_tile[:, :, c * QUARTER:(c + 1) * QUARTER]
+
         for half in range(HALVES):
-            dn_grouped.append(new_d_grouped())
-            nc.scalar.copy(out=write_regrouping(dn_grouped[half][:]), in_=read_regrouping(half_of(dn, half)))
-        n_minus_hid = plane("n_minus_hid")
-        for half in range(HALVES):
-            nc.vector.tensor_tensor(
-                out=half_of(n_minus_hid, half), in0=half_of(n, half), in1=half_of(hid_rows, half),
-                op=ALU.subtract,
-            )
-
-        x_codes = x_mx.tile([P, IN_DIM], U32, align_bytes=64)
-        x_scales = x_mx.tile([P, IN_DIM], U8, align_bytes=64)
-        nc.vector.quantize_mx(
-            out=x_codes[:].bitcast(E4M3_X4),
-            scales=x_scales[:],
-            in_=x_grouped[:].rearrange("p c j -> p (c j)"),
-        )
-
-        multiply_and_store(GATE_N, 0, [quantise(d_grouped) for d_grouped in dn_grouped], vector_is_free=False)
-
-        dz_grouped = []
-        for half in range(HALVES):
-            dz_grouped.append(new_d_grouped())
-            nc.vector.tensor_tensor(
-                out=write_regrouping(dz_grouped[half][:]),
-                in0=read_regrouping(half_of(n_minus_hid, half)),
-                in1=read_regrouping(half_of(gz1z_neg, half)),
-                op=ALU.mult,
-            )
-        multiply_and_store(GATE_Z, 0, [quantise(d_grouped) for d_grouped in dz_grouped], vector_is_free=False)
-
-        r1r_neg = plane("r1r_neg")
-        hn_r1r = plane("hn_r1r")
-        for half in range(HALVES):
-            for k in range(PIECES_PER_HALF):
-                nc.vector.scalar_tensor_tensor(
-                    out=piece_of(r1r_neg, half, k), in0=piece_of(r, half, k), scalar=1.0, in1=piece_of(r, half, k),
-                    op0=ALU.subtract, op1=ALU.mult,
-                )
-            for k in range(PIECES_PER_HALF):
-                nc.vector.scalar_tensor_tensor(
-                    out=piece_of(hn_r1r, half, k), in0=piece_of(hn_rows, half, k), scalar=-1.0,
-                    in1=piece_of(r1r_neg, half, k), op0=ALU.mult, op1=ALU.mult,
-                )
-            d_grouped = new_d_grouped()
-            for k in range(PIECES_PER_HALF):
-                nc.vector.tensor_tensor(
-                    out=write_regrouping(grouped_piece(d_grouped, k)),
-                    in0=read_regrouping(piece_of(dn, half, k)),
-                    in1=read_regrouping(piece_of(hn_r1r, half, k)),
-                    op=ALU.mult,
-                )
-            multiply_and_store(GATE_R, half, [quantise(d_grouped)], vector_is_free=(half == HALVES - 1))
+            pieces = (2 * half, 2 * half + 1)
+            for c in pieces:
+                nc.vector.scalar_tensor_tensor(out=quarter(r1r_neg, c), in0=quarter(r, c), scalar=1.0, in1=quarter(r, c),
+                                               op0=ALU.subtract, op1=ALU.mult)
+            for c in pieces:
+                nc.vector.scalar_tensor_tensor(out=quarter(hn_r1r, c), in0=quarter(hn_rows, c), scalar=-1.0,
+                                               in1=quarter(r1r_neg, c), op0=ALU.mult, op1=ALU.mult)
+            for c in pieces:
+                cols = slice(c * QUARTER, (c + 1) * QUARTER)
+                nc.vector.tensor_tensor(out=write_regrouping(d_r[0][:, cols, :]), in0=read_regrouping(quarter(dn, c)),
+                                        in1=read_regrouping(quarter(hn_r1r, c)), op=ALU.mult)
+            for c in pieces:
+                quantise(d_r, c)
+            multiply_and_store(GATE_R, d_r, (half,), (4, 4) if half == 0 else (4, 2, 1, 1), many_banks=True,
+                               vector_last=(V_LAST if half == 1 else 0))

@@ -30,7 +30,7 @@ BLOCK_WIDTH = IN_DIM // BLOCKS
 RUN = 4
 EIGHTH = 128
 EIGHTHS = HID_DIM // EIGHTH
-N_PE = 6
+N_PE = 4
 QUARTER = 256
 QUARTERS = HID_DIM // QUARTER
 STAGE_SLOTS = 5

@@ -30,7 +30,7 @@ BLOCK_WIDTH = IN_DIM // BLOCKS
 RUN = 4
 EIGHTH = 128
 EIGHTHS = HID_DIM // EIGHTH
-N_PE = 4
+N_PE = 5
 QUARTER = 256
 QUARTERS = HID_DIM // QUARTER
 STAGE_SLOTS = 5
@@ -122,7 +122,9 @@ def tile_grucellv2_v_kernel(tc, x, hid, wx, wh, bx, bh, gates, hn, grad_out, out
         for e in range(N_PE):
             bank = psum_many.tile([P, PACK, EIGHTH], F32, name="bank")
             nmh.append(bank)
-            nc.tensor.matmul(out=bank[:], lhsT=ident[:], rhs=eighth(n, e), start=True, stop=False)
+            nc.tensor.matmul(out=bank[:, 0:2, :], lhsT=ident[:], rhs=eighth(n, e)[:, 0:2, :], start=True, stop=False)
+        for e in range(N_PE):
+            nc.tensor.matmul(out=nmh[e][:, 2:4, :], lhsT=ident[:], rhs=eighth(n, e)[:, 2:4, :], start=False, stop=False)
         for e in range(N_PE):
             nc.tensor.matmul(out=nmh[e][:], lhsT=neg_ident[:], rhs=eighth(hid_rows, e), start=False, stop=True)
 

@@ -206,7 +206,7 @@ def tile_grucellv2_v_kernel(tc, x, hid, wx, wh, bx, bh, gates, hn, grad_out, out
                                 in1=read_regrouping(nmh_v[:]), op=ALU.mult)
         for c in range(QUARTERS):
             quantise(d_z, c)
-        multiply_and_store(GATE_Z, d_z, (0, 1), (2, 2, 2, 2), many_banks=True)
+        multiply_and_store(GATE_Z, d_z, (0, 1), (2, 2, 2, 2), many_banks=False)
 
         d_r = d_tiles("r")
         r1r_neg = z
@@ -229,5 +229,5 @@ def tile_grucellv2_v_kernel(tc, x, hid, wx, wh, bx, bh, gates, hn, grad_out, out
                                         in1=read_regrouping(quarter(hn_r1r, c)), op=ALU.mult)
             for c in pieces:
                 quantise(d_r, c)
-            multiply_and_store(GATE_R, d_r, (half,), (4, 4) if half == 0 else (4, 2, 1, 1), many_banks=True,
+            multiply_and_store(GATE_R, d_r, (half,), (4, 4) if half == 0 else (4, 2, 1, 1), many_banks=(half == 1),
                                vector_last=(V_LAST if half == 1 else 0))

@@ -33,8 +33,9 @@ EIGHTHS = HID_DIM // EIGHTH
 N_PE = 5
 QUARTER = 256
 QUARTERS = HID_DIM // QUARTER
-STAGE_SLOTS = 5
+STAGE_SLOTS = 9
 V_LAST = 8
+HID_FROM = 2
 
 FLOPS = 2 * 3 * TOKENS * IN_DIM * HID_DIM
 BYTES = 3 * TOKENS * 1024 * 2 + 4 * TOKENS * 1024 * 4 + 3 * IN_DIM * HID_DIM * 4
@@ -64,9 +65,10 @@ def tile_grucellv2_v_kernel(tc, x, hid, wx, wh, bx, bh, gates, hn, grad_out, out
         psum_many = ctx.enter_context(tc.psum_pool(name="psum_many", bufs=N_PE))
         ctx.enter_context(tc.manual_schedule())
 
-        x_rows = keep.tile([P, PACK, IN_DIM], BF16)
-        g_rows = keep.tile([P, PACK, HID_DIM], BF16)
-        hid_rows = keep.tile([P, PACK, HID_DIM], BF16)
+        x_rows = stage.tile([P, PACK, IN_DIM], BF16, name="staged", align_bytes=64)
+        g_rows = stage.tile([P, PACK, HID_DIM], BF16, name="staged", align_bytes=64)
+        hid_rows = stage.tile([P, PACK, HID_DIM], BF16, name="staged", align_bytes=64)
+        x_grouped = stage.tile([P, IN_DIM, PACK], BF16, name="staged", align_bytes=64)
         z = keep.tile([P, PACK, HID_DIM], F32)
         n = keep.tile([P, PACK, HID_DIM], F32)
         r = keep.tile([P, PACK, HID_DIM], F32)
@@ -78,8 +80,11 @@ def tile_grucellv2_v_kernel(tc, x, hid, wx, wh, bx, bh, gates, hn, grad_out, out
         for first, last in ((0, 1), (1, 2), (2, 4)):
             load(g_rows, grad_out, first, last)
             load(z, gates[GATE_Z, :, :], first, last)
-        for j in range(PACK):
+        for j in range(PACK - 1):
             load(n, gates[GATE_N, :, :], j, j + 1)
+        for half in range(HALVES):
+            cols = slice(half * N_TILE, (half + 1) * N_TILE)
+            nc.sync.dma_start(out=n[:, PACK - 1, cols], in_=token_rows(gates[GATE_N, :, :])[:, PACK - 1, cols])
         load(x_rows, x, 0, PACK)
         load(hid_rows, hid, 0, PACK)
         load(r, gates[GATE_R, :, :], 0, PACK)
@@ -101,9 +106,9 @@ def tile_grucellv2_v_kernel(tc, x, hid, wx, wh, bx, bh, gates, hn, grad_out, out
         def make_gz(j):
             nc.vector.tensor_tensor(out=gz_neg[:, j, :], in0=z[:, j, :], in1=a_neg[:, j, :], op=ALU.mult)
 
-        def make_dn(j):
-            nc.scalar.activation(out=dn[:, j, :], in_=n[:, j, :], func=ACT.Square)
-            nc.vector.scalar_tensor_tensor(out=dn[:, j, :], in0=dn[:, j, :], scalar=1.0, in1=a_neg[:, j, :],
+        def make_dn(j, cols):
+            nc.scalar.activation(out=dn[:, j, cols], in_=n[:, j, cols], func=ACT.Square)
+            nc.vector.scalar_tensor_tensor(out=dn[:, j, cols], in0=dn[:, j, cols], scalar=1.0, in1=a_neg[:, j, cols],
                                            op0=ALU.subtract, op1=ALU.mult)
 
         make_a(0)
@@ -112,8 +117,10 @@ def tile_grucellv2_v_kernel(tc, x, hid, wx, wh, bx, bh, gates, hn, grad_out, out
         make_gz(1)
         make_a(2)
         make_a(3)
-        for j in range(PACK):
-            make_dn(j)
+        for j in range(PACK - 1):
+            make_dn(j, slice(0, HID_DIM))
+        for half in range(HALVES):
+            make_dn(PACK - 1, slice(half * N_TILE, (half + 1) * N_TILE))
 
         def eighth(rows_tile, e):
             return rows_tile[:, :, e * EIGHTH:(e + 1) * EIGHTH]
@@ -125,17 +132,19 @@ def tile_grucellv2_v_kernel(tc, x, hid, wx, wh, bx, bh, gates, hn, grad_out, out
             nc.tensor.matmul(out=bank[:, 0:2, :], lhsT=ident[:], rhs=eighth(n, e)[:, 0:2, :], start=True, stop=False)
         for e in range(N_PE):
             nc.tensor.matmul(out=nmh[e][:, 2:4, :], lhsT=ident[:], rhs=eighth(n, e)[:, 2:4, :], start=False, stop=False)
-        for e in range(N_PE):
+
+        def subtract_hid(e):
             nc.tensor.matmul(out=nmh[e][:], lhsT=neg_ident[:], rhs=eighth(hid_rows, e), start=False, stop=True)
 
-        x_grouped = keep.tile([P, IN_DIM, PACK], BF16, align_bytes=64)
         x_codes = keep.tile([P, IN_DIM], U32, align_bytes=64)
         x_scales = keep.tile([P, IN_DIM], U8, align_bytes=64)
-        for b in range(BLOCKS):
+
+        def regroup_x(b):
             cols = slice(b * BLOCK_WIDTH, (b + 1) * BLOCK_WIDTH)
             nc.vector.tensor_copy(out=x_grouped[:, cols, :].rearrange("p (t m) j -> p m j t", t=TILES_PER_BLOCK),
                                   in_=x_rows[:, :, cols].rearrange("p j (m t) -> p m j t", t=TILES_PER_BLOCK))
-        for b in range(BLOCKS):
+
+        def quantise_x(b):
             cols = slice(b * BLOCK_WIDTH, (b + 1) * BLOCK_WIDTH)
             nc.vector.quantize_mx(out=x_codes[:, cols].bitcast(E4M3_X4), scales=x_scales[:, cols],
                                   in_=x_grouped[:, cols, :].rearrange("p c j -> p (c j)"))
@@ -156,57 +165,82 @@ def tile_grucellv2_v_kernel(tc, x, hid, wx, wh, bx, bh, gates, hn, grad_out, out
         for half in range(HALVES):
             cols = slice(half * N_TILE, (half + 1) * N_TILE)
             nc.scalar.copy(out=write_regrouping(d_n[0][:, cols, :]), in_=read_regrouping(dn[:, :, cols]))
+        regroup_x(0)
+        regroup_x(1)
+        quantise_x(0)
         quantise(d_n, 0)
         quantise(d_n, 1)
-        make_gz(2)
+        quantise_x(1)
         quantise(d_n, 2)
         quantise(d_n, 3)
+        make_gz(2)
         make_gz(3)
 
-        def multiply_and_store(gate, d, halves, groups, many_banks, vector_last=0):
+        def multiply_and_store(gate, d, halves, chunks, many_banks, vector_last=0, scalar_jobs=None):
             width = len(halves) * N_TILE
             columns = slice(halves[0] * N_TILE, halves[0] * N_TILE + width)
-            idx = 0
+            first_tile = 0
             count = 0
             total = M_TILES * len(halves)
-            for size in groups:
-                staged = stage.tile([P, size, width], F32, name="staged")
-                for k in range(size):
-                    xc = slice(idx * M_TILE, (idx + 1) * M_TILE)
-                    for h, half in enumerate(halves):
+            for stores in chunks:
+                size = sum(stores)
+                places = []
+                for store in stores:
+                    staged = stage.tile([P, store, width], F32, name="staged", align_bytes=64)
+                    for k in range(store):
+                        places.append((staged, k, store))
+                for h, half in enumerate(halves):
+                    dc = slice(half * N_TILE, (half + 1) * N_TILE)
+                    for k in range(size):
+                        for job in (scalar_jobs or {}).get(count, ()):
+                            job()
+                        idx = first_tile + k
+                        xc = slice(idx * M_TILE, (idx + 1) * M_TILE)
                         if many_banks and count % 8 < N_PE:
                             bank = psum_many.tile([P, N_TILE], F32, name="bank")
                         else:
                             bank = psum_few.tile([P, N_TILE], F32, name="bank")
-                        dc = slice(half * N_TILE, (half + 1) * N_TILE)
                         nc.tensor.matmul_mx(out=bank[:], lhsT=x_codes[:, xc].bitcast(E4M3_X4), lhsT_scale=x_scales[:, xc],
                                             rhs=d[1][:, dc].bitcast(E5M2_X4), rhs_scale=d[2][:, dc], start=True, stop=True)
-                        place = staged[:, k, h * N_TILE:(h + 1) * N_TILE]
+                        staged, row, store = places[k]
+                        place = staged[:, row, h * N_TILE:(h + 1) * N_TILE]
                         if count >= total - vector_last and count % 2 == 1:
                             nc.vector.tensor_copy(out=place, in_=bank[:])
                         else:
                             nc.scalar.copy(out=place, in_=bank[:])
                         count += 1
-                    idx += 1
-                first = idx - size
-                b, t = first // TILES_PER_BLOCK, first % TILES_PER_BLOCK
-                nc.sync.dma_start(out=out_blocks[gate, :, b, t:t + size, columns], in_=staged[:])
+                        if h == len(halves) - 1 and row == store - 1:
+                            tile_index = idx - row
+                            b, t = tile_index // TILES_PER_BLOCK, tile_index % TILES_PER_BLOCK
+                            nc.sync.dma_start(out=out_blocks[gate, :, b, t:t + store, columns], in_=staged[:])
+                first_tile += size
 
-        multiply_and_store(GATE_N, d_n, (0, 1), (1, 1, 2, 2, 2), many_banks=False)
+        hid_jobs = {}
+        for e in range(N_PE):
+            hid_jobs[HID_FROM + e] = [lambda e=e: subtract_hid(e)]
+        multiply_and_store(GATE_N, d_n, (0, 1), ((1, 1), (2,), (2,), (2,)), many_banks=False, scalar_jobs=hid_jobs)
 
         d_z = d_tiles("z")
         nmh_v = keep.tile([P, PACK, (EIGHTHS - N_PE) * EIGHTH], F32)
         rest = slice(N_PE * EIGHTH, HID_DIM)
-        nc.vector.tensor_tensor(out=nmh_v[:], in0=n[:, :, rest], in1=hid_rows[:, :, rest], op=ALU.subtract)
-        for e in range(N_PE):
+
+        def make_dz(e):
             cols = slice(e * EIGHTH, (e + 1) * EIGHTH)
             nc.vector.tensor_tensor(out=write_regrouping(d_z[0][:, cols, :]), in0=read_regrouping(gz_neg[:, :, cols]),
                                     in1=read_regrouping(nmh[e][:]), op=ALU.mult)
+
+        for e in range(4):
+            make_dz(e)
+        nc.vector.tensor_tensor(out=nmh_v[:], in0=n[:, :, rest], in1=hid_rows[:, :, rest], op=ALU.subtract)
+        quantise(d_z, 0)
+        quantise(d_z, 1)
+        for e in range(4, N_PE):
+            make_dz(e)
         nc.vector.tensor_tensor(out=write_regrouping(d_z[0][:, rest, :]), in0=read_regrouping(gz_neg[:, :, rest]),
                                 in1=read_regrouping(nmh_v[:]), op=ALU.mult)
-        for c in range(QUARTERS):
-            quantise(d_z, c)
-        multiply_and_store(GATE_Z, d_z, (0, 1), (2, 2, 2, 2), many_banks=False)
+        quantise(d_z, 2)
+        quantise(d_z, 3)
+        multiply_and_store(GATE_Z, d_z, (0, 1), ((2,), (2,), (2,), (2,)), many_banks=False)
 
         d_r = d_tiles("r")
         r1r_neg = z
@@ -229,5 +263,5 @@ def tile_grucellv2_v_kernel(tc, x, hid, wx, wh, bx, bh, gates, hn, grad_out, out
                                         in1=read_regrouping(quarter(hn_r1r, c)), op=ALU.mult)
             for c in pieces:
                 quantise(d_r, c)
-            multiply_and_store(GATE_R, d_r, (half,), (4, 4) if half == 0 else (4, 2, 1, 1), many_banks=(half == 1),
+            multiply_and_store(GATE_R, d_r, (half,), ((4,), (4,)) if half == 0 else ((1,), (1,), (2,), (2,), (2,)), many_banks=(half == 1),
                                vector_last=(V_LAST if half == 1 else 0))

@@ -173,8 +173,9 @@ def tile_grucellv2_v_kernel(tc, x, hid, wx, wh, bx, bh, gates, hn, grad_out, out
         quantise_x(1)
         quantise(d_n, 2)
         quantise(d_n, 3)
-        make_gz(2)
-        make_gz(3)
+        for half in range(HALVES):
+            cols = slice(half * N_TILE, (half + 1) * N_TILE)
+            nc.vector.tensor_tensor(out=gz_neg[:, 2:4, cols], in0=z[:, 2:4, cols], in1=a_neg[:, 2:4, cols], op=ALU.mult)
 
         def multiply_and_store(gate, d, halves, chunks, many_banks, vector_last=0, scalar_jobs=None):
             width = len(halves) * N_TILE
@@ -221,23 +222,23 @@ def tile_grucellv2_v_kernel(tc, x, hid, wx, wh, bx, bh, gates, hn, grad_out, out
         multiply_and_store(GATE_N, d_n, (0, 1), ((1, 1), (2,), (2,), (2,)), many_banks=False, scalar_jobs=hid_jobs)
 
         d_z = d_tiles("z")
-        nmh_v = keep.tile([P, PACK, (EIGHTHS - N_PE) * EIGHTH], F32)
-        rest = slice(N_PE * EIGHTH, HID_DIM)
+        pieces = ((N_PE * EIGHTH, 3 * QUARTER), (3 * QUARTER, HID_DIM))
 
         def make_dz(e):
             cols = slice(e * EIGHTH, (e + 1) * EIGHTH)
             nc.vector.tensor_tensor(out=write_regrouping(d_z[0][:, cols, :]), in0=read_regrouping(gz_neg[:, :, cols]),
                                     in1=read_regrouping(nmh[e][:]), op=ALU.mult)
 
-        for e in range(4):
+        for first, last in pieces:
+            nc.gpsimd.tensor_tensor(out=z[:, :, first:last], in0=n[:, :, first:last], in1=hid_rows[:, :, first:last], op=ALU.subtract)
+        for e in range(N_PE):
             make_dz(e)
-        nc.vector.tensor_tensor(out=nmh_v[:], in0=n[:, :, rest], in1=hid_rows[:, :, rest], op=ALU.subtract)
         quantise(d_z, 0)
         quantise(d_z, 1)
-        for e in range(4, N_PE):
-            make_dz(e)
-        nc.vector.tensor_tensor(out=write_regrouping(d_z[0][:, rest, :]), in0=read_regrouping(gz_neg[:, :, rest]),
-                                in1=read_regrouping(nmh_v[:]), op=ALU.mult)
+        for first, last in pieces:
+            cols = slice(first, last)
+            nc.vector.tensor_tensor(out=write_regrouping(d_z[0][:, cols, :]), in0=read_regrouping(gz_neg[:, :, cols]),
+                                    in1=read_regrouping(z[:, :, cols]), op=ALU.mult)
         quantise(d_z, 2)
         quantise(d_z, 3)
         multiply_and_store(GATE_Z, d_z, (0, 1), ((2,), (2,), (2,), (2,)), many_banks=False)

@@ -77,14 +77,13 @@ def tile_grucellv2_v_kernel(tc, x, hid, wx, wh, bx, bh, gates, hn, grad_out, out
         def load(rows_tile, dram, first, last):
             nc.sync.dma_start(out=rows_tile[:, first:last, :], in_=token_rows(dram)[:, first:last, :])
 
-        for first, last in ((0, 1), (1, 2), (2, 4)):
-            load(g_rows, grad_out, first, last)
-            load(z, gates[GATE_Z, :, :], first, last)
-        for j in range(PACK - 1):
+        load(g_rows, grad_out, 0, 2)
+        load(z, gates[GATE_Z, :, :], 0, 1)
+        load(z, gates[GATE_Z, :, :], 1, 2)
+        load(g_rows, grad_out, 2, 4)
+        load(z, gates[GATE_Z, :, :], 2, 4)
+        for j in range(PACK):
             load(n, gates[GATE_N, :, :], j, j + 1)
-        for half in range(HALVES):
-            cols = slice(half * N_TILE, (half + 1) * N_TILE)
-            nc.sync.dma_start(out=n[:, PACK - 1, cols], in_=token_rows(gates[GATE_N, :, :])[:, PACK - 1, cols])
         load(x_rows, x, 0, PACK)
         load(hid_rows, hid, 0, PACK)
         load(r, gates[GATE_R, :, :], 0, PACK)
@@ -219,7 +218,7 @@ def tile_grucellv2_v_kernel(tc, x, hid, wx, wh, bx, bh, gates, hn, grad_out, out
         hid_jobs = {}
         for e in range(N_PE):
             hid_jobs[HID_FROM + e] = [lambda e=e: subtract_hid(e)]
-        multiply_and_store(GATE_N, d_n, (0, 1), ((1, 1), (2,), (2,), (2,)), many_banks=False, scalar_jobs=hid_jobs)
+        multiply_and_store(GATE_N, d_n, (0, 1), ((2,), (2,), (2,), (2,)), many_banks=False, scalar_jobs=hid_jobs)
 
         d_z = d_tiles("z")
         pieces = ((N_PE * EIGHTH, 3 * QUARTER), (3 * QUARTER, HID_DIM))
@@ -264,5 +263,5 @@ def tile_grucellv2_v_kernel(tc, x, hid, wx, wh, bx, bh, gates, hn, grad_out, out
                                         in1=read_regrouping(quarter(hn_r1r, c)), op=ALU.mult)
             for c in pieces:
                 quantise(d_r, c)
-            multiply_and_store(GATE_R, d_r, (half,), ((4,), (4,)) if half == 0 else ((1,), (1,), (2,), (2,), (2,)), many_banks=(half == 1),
+            multiply_and_store(GATE_R, d_r, (half,), ((4,), (4,)), many_banks=(half == 1),
                                vector_last=(V_LAST if half == 1 else 0))

@@ -263,5 +263,5 @@ def tile_grucellv2_v_kernel(tc, x, hid, wx, wh, bx, bh, gates, hn, grad_out, out
                                         in1=read_regrouping(quarter(hn_r1r, c)), op=ALU.mult)
             for c in pieces:
                 quantise(d_r, c)
-            multiply_and_store(GATE_R, d_r, (half,), ((4,), (4,)), many_banks=(half == 1),
+            multiply_and_store(GATE_R, d_r, (half,), ((4,), (4,)) if half == 0 else ((1,), (1,), (2,), (2,), (2,)), many_banks=(half == 1),
                                vector_last=(V_LAST if half == 1 else 0))

from contextlib import ExitStack

import concourse.mybir as mybir
from concourse.masks import make_identity

F32 = mybir.dt.float32
BF16 = mybir.dt.bfloat16
U32 = mybir.dt.uint32
U8 = mybir.dt.uint8
E4M3_X4 = mybir.dt.float8_e4m3fn_x4
E5M2_X4 = mybir.dt.float8_e5m2_x4
ALU = mybir.AluOpType
ACT = mybir.ActivationFunctionType

P = 128
PACK = 4
TOKENS = P * PACK
IN_DIM = 1024
HID_DIM = 1024
GATE_R = 0
GATE_Z = 1
GATE_N = 2
M_TILE = P
M_TILES = IN_DIM // M_TILE
N_TILE = 512
HALVES = HID_DIM // N_TILE
BLOCKS = 2
TILES_PER_BLOCK = 4
BLOCK_WIDTH = IN_DIM // BLOCKS
RUN = 4
EIGHTH = 128
EIGHTHS = HID_DIM // EIGHTH
N_PE = 5
QUARTER = 256
QUARTERS = HID_DIM // QUARTER
STAGE_SLOTS = 9
V_LAST = 8
HID_FROM = 2

FLOPS = 2 * 3 * TOKENS * IN_DIM * HID_DIM
BYTES = 3 * TOKENS * 1024 * 2 + 4 * TOKENS * 1024 * 4 + 3 * IN_DIM * HID_DIM * 4


def token_rows(dram):
    return dram.rearrange("(p j) c -> p j c", j=PACK)


def read_regrouping(rows):
    return rows.rearrange("p j (c i) -> p c j i", i=RUN)


def write_regrouping(grouped):
    return grouped.rearrange("p (c i) j -> p c j i", i=RUN)


def tile_grucellv2_v_kernel(tc, x, hid, wx, wh, bx, bh, gates, hn, grad_out, out):
    nc = tc.nc
    out_blocks = out.rearrange("g (b m t) h -> g m b t h", b=BLOCKS, t=TILES_PER_BLOCK)

    with ExitStack() as ctx:
        keep = ctx.enter_context(tc.tile_pool(name="keep", bufs=1))
        d_pool = ctx.enter_context(tc.tile_pool(name="d_pool", bufs=2))
        stage = ctx.enter_context(tc.tile_pool(name="stage", bufs=STAGE_SLOTS))
        psum_few = ctx.enter_context(tc.psum_pool(name="psum_few", bufs=8 - N_PE))
        psum_many = ctx.enter_context(tc.psum_pool(name="psum_many", bufs=N_PE))
        ctx.enter_context(tc.manual_schedule())

        x_rows = stage.tile([P, PACK, IN_DIM], BF16, name="staged", align_bytes=64)
        g_rows = stage.tile([P, PACK, HID_DIM], BF16, name="staged", align_bytes=64)
        hid_rows = stage.tile([P, PACK, HID_DIM], BF16, name="staged", align_bytes=64)
        x_grouped = stage.tile([P, IN_DIM, PACK], BF16, name="staged", align_bytes=64)
        z = keep.tile([P, PACK, HID_DIM], F32)
        n = keep.tile([P, PACK, HID_DIM], F32)
        r = keep.tile([P, PACK, HID_DIM], F32)
        hn_rows = keep.tile([P, PACK, HID_DIM], F32)

        def load(rows_tile, dram, first, last):
            nc.sync.dma_start(out=rows_tile[:, first:last, :], in_=token_rows(dram)[:, first:last, :])

        load(g_rows, grad_out, 0, 2)
        load(z, gates[GATE_Z, :, :], 0, 1)
        load(z, gates[GATE_Z, :, :], 1, 2)
        load(g_rows, grad_out, 2, 4)
        load(z, gates[GATE_Z, :, :], 2, 4)
        for j in range(PACK):
            load(n, gates[GATE_N, :, :], j, j + 1)
        load(x_rows, x, 0, PACK)
        load(hid_rows, hid, 0, PACK)
        load(r, gates[GATE_R, :, :], 0, PACK)
        load(hn_rows, hn, 0, PACK)

        ident = keep.tile([P, P], F32)
        make_identity(nc, ident[:])
        neg_ident = keep.tile([P, P], BF16)
        nc.gpsimd.tensor_scalar(out=neg_ident[:], in0=ident[:], scalar1=-1.0, scalar2=0.0, op0=ALU.mult, op1=ALU.add)

        a_neg = keep.tile([P, PACK, HID_DIM], F32)
        gz_neg = keep.tile([P, PACK, HID_DIM], F32)
        dn = keep.tile([P, PACK, HID_DIM], F32)

        def make_a(j):
            nc.vector.scalar_tensor_tensor(out=a_neg[:, j, :], in0=z[:, j, :], scalar=1.0, in1=g_rows[:, j, :],
                                           op0=ALU.subtract, op1=ALU.mult)

        def make_gz(j):
            nc.vector.tensor_tensor(out=gz_neg[:, j, :], in0=z[:, j, :], in1=a_neg[:, j, :], op=ALU.mult)

        def make_dn(j, cols):
            nc.scalar.activation(out=dn[:, j, cols], in_=n[:, j, cols], func=ACT.Square)
            nc.vector.scalar_tensor_tensor(out=dn[:, j, cols], in0=dn[:, j, cols], scalar=1.0, in1=a_neg[:, j, cols],
                                           op0=ALU.subtract, op1=ALU.mult)

        make_a(0)
        make_a(1)
        make_gz(0)
        make_gz(1)
        make_a(2)
        make_a(3)
        for j in range(PACK - 1):
            make_dn(j, slice(0, HID_DIM))
        for half in range(HALVES):
            make_dn(PACK - 1, slice(half * N_TILE, (half + 1) * N_TILE))

        def eighth(rows_tile, e):
            return rows_tile[:, :, e * EIGHTH:(e + 1) * EIGHTH]

        nmh = []
        for e in range(N_PE):
            bank = psum_many.tile([P, PACK, EIGHTH], F32, name="bank")
            nmh.append(bank)
            nc.tensor.matmul(out=bank[:, 0:2, :], lhsT=ident[:], rhs=eighth(n, e)[:, 0:2, :], start=True, stop=False)
        for e in range(N_PE):
            nc.tensor.matmul(out=nmh[e][:, 2:4, :], lhsT=ident[:], rhs=eighth(n, e)[:, 2:4, :], start=False, stop=False)

        def subtract_hid(e):
            nc.tensor.matmul(out=nmh[e][:], lhsT=neg_ident[:], rhs=eighth(hid_rows, e), start=False, stop=True)

        x_codes = keep.tile([P, IN_DIM], U32, align_bytes=64)
        x_scales = keep.tile([P, IN_DIM], U8, align_bytes=64)

        def regroup_x(b):
            cols = slice(b * BLOCK_WIDTH, (b + 1) * BLOCK_WIDTH)
            nc.vector.tensor_copy(out=x_grouped[:, cols, :].rearrange("p (t m) j -> p m j t", t=TILES_PER_BLOCK),
                                  in_=x_rows[:, :, cols].rearrange("p j (m t) -> p m j t", t=TILES_PER_BLOCK))

        def quantise_x(b):
            cols = slice(b * BLOCK_WIDTH, (b + 1) * BLOCK_WIDTH)
            nc.vector.quantize_mx(out=x_codes[:, cols].bitcast(E4M3_X4), scales=x_scales[:, cols],
                                  in_=x_grouped[:, cols, :].rearrange("p c j -> p (c j)"))

        def d_tiles(name):
            grouped = d_pool.tile([P, HID_DIM, PACK], BF16, name="grouped", align_bytes=64)
            codes = keep.tile([P, HID_DIM], U32, name="codes_" + name, align_bytes=64)
            scales = keep.tile([P, HID_DIM], U8, name="scales_" + name, align_bytes=64)
            return grouped, codes, scales

        def quantise(d, c):
            grouped, codes, scales = d
            cols = slice(c * QUARTER, (c + 1) * QUARTER)
            nc.vector.quantize_mx(out=codes[:, cols].bitcast(E5M2_X4), scales=scales[:, cols],
                                  in_=grouped[:, cols, :].rearrange("p c j -> p (c j)"))

        d_n = d_tiles("n")
        for half in range(HALVES):
            cols = slice(half * N_TILE, (half + 1) * N_TILE)
            nc.scalar.copy(out=write_regrouping(d_n[0][:, cols, :]), in_=read_regrouping(dn[:, :, cols]))
        regroup_x(0)
        regroup_x(1)
        quantise_x(0)
        quantise(d_n, 0)
        quantise(d_n, 1)
        quantise_x(1)
        quantise(d_n, 2)
        quantise(d_n, 3)
        for half in range(HALVES):
            cols = slice(half * N_TILE, (half + 1) * N_TILE)
            nc.vector.tensor_tensor(out=gz_neg[:, 2:4, cols], in0=z[:, 2:4, cols], in1=a_neg[:, 2:4, cols], op=ALU.mult)

        def multiply_and_store(gate, d, halves, chunks, many_banks, vector_last=0, scalar_jobs=None):
            width = len(halves) * N_TILE
            columns = slice(halves[0] * N_TILE, halves[0] * N_TILE + width)
            first_tile = 0
            count = 0
            total = M_TILES * len(halves)
            for stores in chunks:
                size = sum(stores)
                places = []
                for store in stores:
                    staged = stage.tile([P, store, width], F32, name="staged", align_bytes=64)
                    for k in range(store):
                        places.append((staged, k, store))
                for h, half in enumerate(halves):
                    dc = slice(half * N_TILE, (half + 1) * N_TILE)
                    for k in range(size):
                        for job in (scalar_jobs or {}).get(count, ()):
                            job()
                        idx = first_tile + k
                        xc = slice(idx * M_TILE, (idx + 1) * M_TILE)
                        if many_banks and count % 8 < N_PE:
                            bank = psum_many.tile([P, N_TILE], F32, name="bank")
                        else:
                            bank = psum_few.tile([P, N_TILE], F32, name="bank")
                        nc.tensor.matmul_mx(out=bank[:], lhsT=x_codes[:, xc].bitcast(E4M3_X4), lhsT_scale=x_scales[:, xc],
                                            rhs=d[1][:, dc].bitcast(E5M2_X4), rhs_scale=d[2][:, dc], start=True, stop=True)
                        staged, row, store = places[k]
                        place = staged[:, row, h * N_TILE:(h + 1) * N_TILE]
                        if count >= total - vector_last and count % 2 == 1:
                            nc.vector.tensor_copy(out=place, in_=bank[:])
                        else:
                            nc.scalar.copy(out=place, in_=bank[:])
                        count += 1
                        if h == len(halves) - 1 and row == store - 1:
                            tile_index = idx - row
                            b, t = tile_index // TILES_PER_BLOCK, tile_index % TILES_PER_BLOCK
                            nc.sync.dma_start(out=out_blocks[gate, :, b, t:t + store, columns], in_=staged[:])
                first_tile += size

        hid_jobs = {}
        for e in range(N_PE):
            hid_jobs[HID_FROM + e] = [lambda e=e: subtract_hid(e)]
        multiply_and_store(GATE_N, d_n, (0, 1), ((2,), (2,), (2,), (2,)), many_banks=False, scalar_jobs=hid_jobs)

        d_z = d_tiles("z")
        pieces = ((N_PE * EIGHTH, 3 * QUARTER), (3 * QUARTER, HID_DIM))

        def make_dz(e):
            cols = slice(e * EIGHTH, (e + 1) * EIGHTH)
            nc.vector.tensor_tensor(out=write_regrouping(d_z[0][:, cols, :]), in0=read_regrouping(gz_neg[:, :, cols]),
                                    in1=read_regrouping(nmh[e][:]), op=ALU.mult)

        for first, last in pieces:
            nc.gpsimd.tensor_tensor(out=z[:, :, first:last], in0=n[:, :, first:last], in1=hid_rows[:, :, first:last], op=ALU.subtract)
        for e in range(N_PE):
            make_dz(e)
        quantise(d_z, 0)
        quantise(d_z, 1)
        for first, last in pieces:
            cols = slice(first, last)
            nc.vector.tensor_tensor(out=write_regrouping(d_z[0][:, cols, :]), in0=read_regrouping(gz_neg[:, :, cols]),
                                    in1=read_regrouping(z[:, :, cols]), op=ALU.mult)
        quantise(d_z, 2)
        quantise(d_z, 3)
        multiply_and_store(GATE_Z, d_z, (0, 1), ((2,), (2,), (2,), (2,)), many_banks=False)

        d_r = d_tiles("r")
        r1r_neg = z
        hn_r1r = a_neg

        def quarter(rows_tile, c):
            return rows_tile[:, :, c * QUARTER:(c + 1) * QUARTER]

        for half in range(HALVES):
            pieces = (2 * half, 2 * half + 1)
            for c in pieces:
                nc.vector.scalar_tensor_tensor(out=quarter(r1r_neg, c), in0=quarter(r, c), scalar=1.0, in1=quarter(r, c),
                                               op0=ALU.subtract, op1=ALU.mult)
            for c in pieces:
                nc.vector.scalar_tensor_tensor(out=quarter(hn_r1r, c), in0=quarter(hn_rows, c), scalar=-1.0,
                                               in1=quarter(r1r_neg, c), op0=ALU.mult, op1=ALU.mult)
            for c in pieces:
                cols = slice(c * QUARTER, (c + 1) * QUARTER)
                nc.vector.tensor_tensor(out=write_regrouping(d_r[0][:, cols, :]), in0=read_regrouping(quarter(dn, c)),
                                        in1=read_regrouping(quarter(hn_r1r, c)), op=ALU.mult)
            for c in pieces:
                quantise(d_r, c)
            multiply_and_store(GATE_R, d_r, (half,), ((4,), (4,)) if half == 0 else ((1,), (1,), (2,), (2,), (2,)), many_banks=(half == 1),
                               vector_last=(V_LAST if half == 1 else 0))
